import numpy as np
import ml_dtypes


def mxq(x, axis, fmt="e4m3"):
    dtype, down = {"e4m3": (ml_dtypes.float8_e4m3fn, 7), "e5m2": (ml_dtypes.float8_e5m2, 14)}[fmt]
    v = np.moveaxis(np.asarray(x, np.float32).astype(ml_dtypes.bfloat16).astype(np.float64), axis, -1)
    blocks = v.reshape(v.shape[:-1] + (-1, 32))
    amax = np.abs(blocks).max(-1, keepdims=True)
    byte = np.maximum(np.where(amax > 0, np.frexp(amax)[1] - 1 + 127, 0) - down, 1)
    scale = np.exp2(byte - 127.0)
    codes = (blocks / scale).astype(np.float32).astype(dtype).astype(np.float64)
    return np.moveaxis((codes * scale).reshape(v.shape), -1, axis)


WIDE = False


def mx_kscale(k):
    if not WIDE:
        return np.ones(k)
    levels = np.array([10, -10, 5, -5, 0])
    a = np.random.permutation(np.resize(levels, k // 512 * 4)).reshape(k // 512, 4)
    idx = np.arange(k)
    return np.exp2(a[idx // 512, idx % 128 // 32])


BF16 = ml_dtypes.bfloat16


def bf(x):
    return np.asarray(x, np.float32).astype(BF16)


def f64(x):
    return np.asarray(x).astype(np.float64)


B, C, DW, F1, F2, G, J = 512, 512, 300, 1024, 2048, 2048, 2048
SLOPE = 0.2
PE = 2.0 / np.sqrt(C)


def leaky_relu(v):
    return np.where(v >= 0.0, v, SLOPE * v)


def gen_adj(a):
    d = a.sum(1) ** -0.5
    return d[:, None] * a.T * d[None, :]


def setup_inputs():
    s = mx_kscale(F1)
    return {"x_pre": bf(np.random.standard_normal((C, F1)) * s),
            "A": bf(np.random.uniform(size=(C, C)) * (np.random.uniform(size=(C, C)) < PE)),
            "W_gc2": bf(np.random.standard_normal((F1, F2)) * 2.6 / np.sqrt(F1) / s[:, None])}


def reference(x_pre, A, W_gc2):
    adj = gen_adj(f64(A))
    h = leaky_relu(f64(x_pre))
    support = mxq(h, 1, "e4m3") @ mxq(f64(W_gc2), 0, "e4m3")
    return mxq(adj, 1, "e4m3") @ mxq(support, 0, "e4m3")

@@ -1,0 +1,217 @@
+from contextlib import ExitStack
+
+import concourse.mybir as mybir
+from concourse.masks import make_identity
+
+FLOPS = 2 * 512 * 1024 * 2048 + 2 * 512 * 512 * 2048
+
+BF16 = mybir.dt.bfloat16
+F32 = mybir.dt.float32
+U32 = mybir.dt.uint32
+U8 = mybir.dt.uint8
+FP8X4 = mybir.dt.float8_e4m3fn_x4
+ACT = mybir.ActivationFunctionType
+ALU = mybir.AluOpType
+
+P = 128
+PACK = 4
+NODES = 512
+K1 = 1024
+F2 = 2048
+PASSES1 = K1 // (P * PACK)
+NT = NODES // P
+FC = 512
+NCH = F2 // FC
+FB = 128
+NFB = FC // FB
+SLOPE = 0.2
+
+
+def tile_gcnresnet_pa_kernel(tc, x_pre, A, W_gc2, out):
+    nc = tc.nc
+    with ExitStack() as ctx:
+        const = ctx.enter_context(tc.tile_pool(name="const", bufs=1))
+        work = ctx.enter_context(tc.tile_pool(name="work", bufs=2))
+        wraw = ctx.enter_context(tc.tile_pool(name="wraw", bufs=NCH))
+        wq = ctx.enter_context(tc.tile_pool(name="wq", bufs=2))
+        outp = ctx.enter_context(tc.tile_pool(name="outp", bufs=2))
+        psum = ctx.enter_context(tc.psum_pool(name="psum", bufs=4))
+
+        def copy_on(engine, dst, src):
+            if engine == "v":
+                nc.vector.tensor_copy(out=dst, in_=src)
+            else:
+                nc.scalar.copy(out=dst, in_=src)
+
+        ident_b = const.tile([P, P], BF16, name="ident_b")
+        make_identity(nc, ident_b[:])
+        ident_f = const.tile([P, P], F32, name="ident_f")
+        make_identity(nc, ident_f[:])
+        one = const.tile([P, 1], F32, name="one")
+        nc.vector.memset(one[:], 1.0)
+        warm = const.tile([P, 1], F32, name="warm")
+        nc.scalar.activation(out=warm[:], in_=one[:], func=ACT.Sqrt)
+
+        x_raw = const.tile([P, NT, K1], BF16, name="x_raw")
+        x_view = x_pre.rearrange("(p t) k -> p t k", t=NT)
+        for t in range(NT):
+            nc.sync.dma_start(out=x_raw[:, t, :], in_=x_view[:, t, :])
+        w_view = W_gc2.rearrange("(g p) f -> p g f", p=P)
+        a_raw = const.tile([P, NT, NODES], BF16, name="a_raw")
+        w_raw = []
+        for n in range(NCH):
+            w_tile = wraw.tile([P, PASSES1 * PACK, FC], BF16, name="w_raw", tag="w_raw")
+            nc.sync.dma_start(out=w_tile[:], in_=w_view[:, :, n * FC:(n + 1) * FC])
+            w_raw.append(w_tile)
+            if n == 0:
+                nc.sync.dma_start(out=a_raw[:], in_=A.rearrange("(p t) i -> p t i", t=NT))
+
+        h_nat = const.tile([P, NT, K1], BF16, name="h_nat")
+        h_grp = const.tile([P, NT, PASSES1, P, PACK], BF16, name="h_grp", align_bytes=64)
+        h_code = const.tile([P, NT, PASSES1 * P], U32, name="h_code", align_bytes=64)
+        h_scale = const.tile([P, NT, PASSES1 * P], U8, name="h_scale", align_bytes=64)
+        for t in range(NT):
+            scaled = work.tile([P, K1], BF16, name="scaled", tag="scaled")
+            nc.vector.tensor_scalar_mul(out=scaled[:], in0=x_raw[:, t, :], scalar1=SLOPE)
+            nc.vector.tensor_max(out=h_nat[:, t, :], in0=x_raw[:, t, :], in1=scaled[:])
+            for c in range(PASSES1):
+                xt = psum.tile([P, PACK, P], BF16, name="xt", tag="s1" if c == 0 else "s2")
+                for j in range(PACK):
+                    k0 = (c * PACK + j) * P
+                    nc.tensor.transpose(out=xt[:, j, :], in_=h_nat[:, t, k0:k0 + P], identity=ident_b[:])
+                copy_on("s", h_grp[:, t, c, :, :], xt[:].rearrange("p j m -> p m j"))
+
+        w_code = {}
+        w_scale = {}
+
+        def prep_w(n):
+            grp = work.tile([P, PASSES1, FC, PACK], BF16, name="w_grp", tag="w_grp", align_bytes=64)
+            code = wq.tile([P, PASSES1, FC], U32, name="w_code", tag="w_code", align_bytes=64)
+            scale = wq.tile([P, PASSES1, FC], U8, name="w_scale", tag="w_scale", align_bytes=64)
+            for c in range(PASSES1):
+                nc.vector.tensor_copy(
+                    out=grp[:, c, :, :].rearrange("p (o i) j -> p o j i", i=4),
+                    in_=w_raw[n][:, c * PACK:(c + 1) * PACK, :].rearrange("p j (o i) -> p o j i", i=4),
+                )
+            for c in range(PASSES1):
+                nc.vector.quantize_mx(
+                    out=code[:, c, :].bitcast(FP8X4),
+                    scales=scale[:, c, :],
+                    in_=grp[:, c, :, :].rearrange("p f j -> p (f j)"),
+                )
+            w_code[n] = code
+            w_scale[n] = scale
+
+        def quant_h(t):
+            nc.vector.quantize_mx(
+                out=h_code[:, t, :].bitcast(FP8X4),
+                scales=h_scale[:, t, :],
+                in_=h_grp[:, t, :, :, :].rearrange("p c m j -> p (c m j)"),
+            )
+
+        for t in range(NT):
+            quant_h(t)
+        prep_w(0)
+
+        rowsum = const.tile([P, NT], F32, name="rowsum")
+        junk = const.tile([P, NODES], BF16, name="junk")
+        for t in range(NT):
+            nc.scalar.activation(out=junk[:], in_=a_raw[:, t, :], func=ACT.Copy, accum_out=rowsum[:, t:t + 1])
+        root = const.tile([P, NT], F32, name="root")
+        nc.scalar.activation(out=root[:], in_=rowsum[:], func=ACT.Sqrt)
+        d_col = const.tile([P, NT], F32, name="d_col")
+        nc.vector.reciprocal(out=d_col[:], in_=root[:])
+
+        sup_grp = {}
+        sup_code = {}
+        sup_scale = {}
+        banks1 = {}
+
+        def stage1(n):
+            for fb in range(NFB):
+                acc = psum.tile([P, NT, FB], F32, name="acc1", tag="s1")
+                for t in range(NT):
+                    for c in range(PASSES1):
+                        nc.tensor.matmul_mx(
+                            out=acc[:, t, :],
+                            lhsT=h_code[:, t, c * P:(c + 1) * P].bitcast(FP8X4),
+                            lhsT_scale=h_scale[:, t, c * P:(c + 1) * P],
+                            rhs=w_code[n][:, c, fb * FB:(fb + 1) * FB].bitcast(FP8X4),
+                            rhs_scale=w_scale[n][:, c, fb * FB:(fb + 1) * FB],
+                            start=(c == 0),
+                            stop=(c == PASSES1 - 1),
+                        )
+                banks1[(n, fb)] = acc
+
+        def drain1(n, engines):
+            grp = work.tile([P, FC, NT], BF16, name="sup_grp", tag="sup_grp", align_bytes=64)
+            for fb in range(NFB):
+                copy_on(engines[fb], grp[:, fb * FB:(fb + 1) * FB, :], banks1[(n, fb)][:].rearrange("p t f -> p f t"))
+            sup_grp[n] = grp
+
+        def quant_sup(n):
+            code = wq.tile([P, FC], U32, name="sup_code", tag="sup_code", align_bytes=64)
+            scale = wq.tile([P, FC], U8, name="sup_scale", tag="sup_scale", align_bytes=64)
+            nc.vector.quantize_mx(
+                out=code[:].bitcast(FP8X4), scales=scale[:], in_=sup_grp[n][:].rearrange("p f t -> p (f t)")
+            )
+            sup_code[n] = code
+            sup_scale[n] = scale
+
+        stage1(0)
+
+        d_all = psum.tile([P, NT, P], F32, name="d_all", tag="s2")
+        for t in range(NT):
+            nc.tensor.matmul(
+                out=d_all[:, t, :], lhsT=d_col[:, t:t + 1].to_broadcast([P, P]), rhs=ident_f[:], start=True, stop=True
+            )
+        prep_w(1)
+        adj_pl = const.tile([P, NT, NODES], BF16, name="adj_pl")
+        for t in range(NT):
+            nc.vector.scalar_tensor_tensor(
+                out=adj_pl[:, t, :].rearrange("p (n u) -> p n u", u=NT),
+                in0=a_raw[:, t, :].rearrange("p (n u) -> p n u", u=NT),
+                scalar=d_col[:, t:t + 1],
+                in1=d_all[:].rearrange("p u n -> p n u"),
+                op0=ALU.mult,
+                op1=ALU.mult,
+            )
+        adj_grp = const.tile([P, NODES, NT], BF16, name="adj_grp", align_bytes=64)
+        nc.vector.tensor_copy(
+            out=adj_grp[:].rearrange("p (o i) t -> p o t i", i=4),
+            in_=adj_pl[:].rearrange("p t (o i) -> p o t i", i=4),
+        )
+        adj_code = const.tile([P, NODES], U32, name="adj_code", align_bytes=64)
+        adj_scale = const.tile([P, NODES], U8, name="adj_scale", align_bytes=64)
+
+        drain1(0, "ssss")
+        nc.vector.quantize_mx(
+            out=adj_code[:].bitcast(FP8X4), scales=adj_scale[:], in_=adj_grp[:].rearrange("p i t -> p (i t)")
+        )
+        quant_sup(0)
+
+        def stage2(n, engines):
+            res = outp.tile([P, NT, FC], F32, name="res", tag="res")
+            for it in range(NT):
+                acc = psum.tile([P, FC], F32, name="acc2", tag="s2")
+                nc.tensor.matmul_mx(
+                    out=acc[:],
+                    lhsT=adj_code[:, it * P:(it + 1) * P].bitcast(FP8X4),
+                    lhsT_scale=adj_scale[:, it * P:(it + 1) * P],
+                    rhs=sup_code[n][:].bitcast(FP8X4),
+                    rhs_scale=sup_scale[n][:],
+                    start=True,
+                    stop=True,
+                )
+                copy_on(engines[it], res[:, it, :], acc[:])
+                nc.sync.dma_start(out=out[it * P:(it + 1) * P, n * FC:(n + 1) * FC], in_=res[:, it, :])
+
+        for n in range(NCH):
+            if n + 1 < NCH:
+                stage1(n + 1)
+                drain1(n + 1, "ssss" if n + 2 < NCH else "svsv")
+            if n + 2 < NCH:
+                prep_w(n + 2)
+            stage2(n, "ssss" if n + 1 < NCH else "svsv")
+            if n + 1 < NCH:
+                quant_sup(n + 1)

@@ -22,20 +22,22 @@ PASSES1 = K1 // (P * PACK)
 NT = NODES // P
 FC = 512
 NCH = F2 // FC
+FU = 256
 FB = 128
-NFB = FC // FB
 SLOPE = 0.2
+GROUPS = ((0, 1), (2, 3), (4, 5), (6,), (7,))
 
 
 def tile_gcnresnet_pa_kernel(tc, x_pre, A, W_gc2, out):
     nc = tc.nc
     with ExitStack() as ctx:
         const = ctx.enter_context(tc.tile_pool(name="const", bufs=1))
-        work = ctx.enter_context(tc.tile_pool(name="work", bufs=2))
+        work = ctx.enter_context(tc.tile_pool(name="work", bufs=3))
         wraw = ctx.enter_context(tc.tile_pool(name="wraw", bufs=NCH))
-        wq = ctx.enter_context(tc.tile_pool(name="wq", bufs=2))
-        outp = ctx.enter_context(tc.tile_pool(name="outp", bufs=2))
+        wq = ctx.enter_context(tc.tile_pool(name="wq", bufs=4))
+        outp = ctx.enter_context(tc.tile_pool(name="outp", bufs=8))
         psum = ctx.enter_context(tc.psum_pool(name="psum", bufs=4))
+        ctx.enter_context(tc.manual_schedule())
 
         def copy_on(engine, dst, src):
             if engine == "v":
@@ -70,148 +72,304 @@ def tile_gcnresnet_pa_kernel(tc, x_pre, A, W_gc2, out):
         h_grp = const.tile([P, NT, PASSES1, P, PACK], BF16, name="h_grp", align_bytes=64)
         h_code = const.tile([P, NT, PASSES1 * P], U32, name="h_code", align_bytes=64)
         h_scale = const.tile([P, NT, PASSES1 * P], U8, name="h_scale", align_bytes=64)
-        for t in range(NT):
+        xts = {}
+        scaleds = {}
+
+        def ts(t):
             scaled = work.tile([P, K1], BF16, name="scaled", tag="scaled")
             nc.vector.tensor_scalar_mul(out=scaled[:], in0=x_raw[:, t, :], scalar1=SLOPE)
-            nc.vector.tensor_max(out=h_nat[:, t, :], in0=x_raw[:, t, :], in1=scaled[:])
+            scaleds[t] = scaled
+
+        def tt(t):
+            nc.vector.tensor_max(out=h_nat[:, t, :], in0=x_raw[:, t, :], in1=scaleds[t][:])
+
+        def transp(t):
             for c in range(PASSES1):
                 xt = psum.tile([P, PACK, P], BF16, name="xt", tag="s1" if c == 0 else "s2")
                 for j in range(PACK):
                     k0 = (c * PACK + j) * P
                     nc.tensor.transpose(out=xt[:, j, :], in_=h_nat[:, t, k0:k0 + P], identity=ident_b[:])
-                copy_on("s", h_grp[:, t, c, :, :], xt[:].rearrange("p j m -> p m j"))
+                xts[(t, c)] = xt
 
-        w_code = {}
-        w_scale = {}
+        def hco(t, c, engine):
+            copy_on(engine, h_grp[:, t, c, :, :], xts[(t, c)][:].rearrange("p j m -> p m j"))
 
-        def prep_w(n):
-            grp = work.tile([P, PASSES1, FC, PACK], BF16, name="w_grp", tag="w_grp", align_bytes=64)
-            code = wq.tile([P, PASSES1, FC], U32, name="w_code", tag="w_code", align_bytes=64)
-            scale = wq.tile([P, PASSES1, FC], U8, name="w_scale", tag="w_scale", align_bytes=64)
-            for c in range(PASSES1):
-                nc.vector.tensor_copy(
-                    out=grp[:, c, :, :].rearrange("p (o i) j -> p o j i", i=4),
-                    in_=w_raw[n][:, c * PACK:(c + 1) * PACK, :].rearrange("p j (o i) -> p o j i", i=4),
-                )
-            for c in range(PASSES1):
-                nc.vector.quantize_mx(
-                    out=code[:, c, :].bitcast(FP8X4),
-                    scales=scale[:, c, :],
-                    in_=grp[:, c, :, :].rearrange("p f j -> p (f j)"),
-                )
-            w_code[n] = code
-            w_scale[n] = scale
-
-        def quant_h(t):
+        def qh(t):
             nc.vector.quantize_mx(
                 out=h_code[:, t, :].bitcast(FP8X4),
                 scales=h_scale[:, t, :],
                 in_=h_grp[:, t, :, :, :].rearrange("p c m j -> p (c m j)"),
             )
 
-        for t in range(NT):
-            quant_h(t)
-        prep_w(0)
+        w_grp = {}
+        w_code = {}
+        w_scale = {}
+
+        def rg(u, engine):
+            grp = work.tile([P, PASSES1, FU, PACK], BF16, name="w_grp", tag="w_grp", align_bytes=64)
+            src = w_raw[u // 2][:, :, (u % 2) * FU:(u % 2 + 1) * FU]
+            if engine == "v":
+                nc.vector.tensor_copy(
+                    out=grp[:].rearrange("p c (o i) j -> p c o j i", i=4),
+                    in_=src.rearrange("p (c j) (o i) -> p c o j i", j=PACK, i=4),
+                )
+            else:
+                for c in range(PASSES1):
+                    nc.scalar.copy(
+                        out=grp[:, c, :, :].rearrange("p (o i) j -> p o j i", i=4),
+                        in_=src[:, c * PACK:(c + 1) * PACK, :].rearrange("p j (o i) -> p o j i", i=4),
+                    )
+            w_grp[u] = grp
+
+        def qw(u):
+            code = wq.tile([P, PASSES1, FU], U32, name="w_code", tag="w_code", align_bytes=64)
+            scale = wq.tile([P, PASSES1, FU], U8, name="w_scale", tag="w_scale", align_bytes=64)
+            nc.vector.quantize_mx(
+                out=code[:].rearrange("p c f -> p (c f)").bitcast(FP8X4),
+                scales=scale[:].rearrange("p c f -> p (c f)"),
+                in_=w_grp[u][:].rearrange("p c f j -> p (c f j)"),
+            )
+            w_code[u] = code
+            w_scale[u] = scale
 
         rowsum = const.tile([P, NT], F32, name="rowsum")
         junk = const.tile([P, NODES], BF16, name="junk")
-        for t in range(NT):
-            nc.scalar.activation(out=junk[:], in_=a_raw[:, t, :], func=ACT.Copy, accum_out=rowsum[:, t:t + 1])
         root = const.tile([P, NT], F32, name="root")
-        nc.scalar.activation(out=root[:], in_=rowsum[:], func=ACT.Sqrt)
         d_col = const.tile([P, NT], F32, name="d_col")
-        nc.vector.reciprocal(out=d_col[:], in_=root[:])
-
-        sup_grp = {}
-        sup_code = {}
-        sup_scale = {}
-        banks1 = {}
-
-        def stage1(n):
-            for fb in range(NFB):
-                acc = psum.tile([P, NT, FB], F32, name="acc1", tag="s1")
-                for t in range(NT):
-                    for c in range(PASSES1):
-                        nc.tensor.matmul_mx(
-                            out=acc[:, t, :],
-                            lhsT=h_code[:, t, c * P:(c + 1) * P].bitcast(FP8X4),
-                            lhsT_scale=h_scale[:, t, c * P:(c + 1) * P],
-                            rhs=w_code[n][:, c, fb * FB:(fb + 1) * FB].bitcast(FP8X4),
-                            rhs_scale=w_scale[n][:, c, fb * FB:(fb + 1) * FB],
-                            start=(c == 0),
-                            stop=(c == PASSES1 - 1),
-                        )
-                banks1[(n, fb)] = acc
-
-        def drain1(n, engines):
-            grp = work.tile([P, FC, NT], BF16, name="sup_grp", tag="sup_grp", align_bytes=64)
-            for fb in range(NFB):
-                copy_on(engines[fb], grp[:, fb * FB:(fb + 1) * FB, :], banks1[(n, fb)][:].rearrange("p t f -> p f t"))
-            sup_grp[n] = grp
-
-        def quant_sup(n):
-            code = wq.tile([P, FC], U32, name="sup_code", tag="sup_code", align_bytes=64)
-            scale = wq.tile([P, FC], U8, name="sup_scale", tag="sup_scale", align_bytes=64)
-            nc.vector.quantize_mx(
-                out=code[:].bitcast(FP8X4), scales=scale[:], in_=sup_grp[n][:].rearrange("p f t -> p (f t)")
-            )
-            sup_code[n] = code
-            sup_scale[n] = scale
-
-        stage1(0)
-
-        d_all = psum.tile([P, NT, P], F32, name="d_all", tag="s2")
-        for t in range(NT):
-            nc.tensor.matmul(
-                out=d_all[:, t, :], lhsT=d_col[:, t:t + 1].to_broadcast([P, P]), rhs=ident_f[:], start=True, stop=True
-            )
-        prep_w(1)
         adj_pl = const.tile([P, NT, NODES], BF16, name="adj_pl")
-        for t in range(NT):
+        adj_grp = const.tile([P, NODES, NT], BF16, name="adj_grp", align_bytes=64)
+        adj_code = const.tile([P, NODES], U32, name="adj_code", align_bytes=64)
+        adj_scale = const.tile([P, NODES], U8, name="adj_scale", align_bytes=64)
+        d_alls = {}
+
+        def rs(t):
+            nc.scalar.activation(out=junk[:], in_=a_raw[:, t, :], func=ACT.Copy, accum_out=rowsum[:, t:t + 1])
+
+        def sqrt():
+            nc.scalar.activation(out=root[:], in_=rowsum[:], func=ACT.Sqrt)
+
+        def recip():
+            nc.vector.reciprocal(out=d_col[:], in_=root[:])
+
+        def bc():
+            d_all = psum.tile([P, NT, P], F32, name="d_all", tag="s2")
+            for t in range(NT):
+                nc.tensor.matmul(
+                    out=d_all[:, t, :], lhsT=d_col[:, t:t + 1].to_broadcast([P, P]), rhs=ident_f[:], start=True, stop=True
+                )
+            d_alls[0] = d_all
+
+        def stt(t):
             nc.vector.scalar_tensor_tensor(
                 out=adj_pl[:, t, :].rearrange("p (n u) -> p n u", u=NT),
                 in0=a_raw[:, t, :].rearrange("p (n u) -> p n u", u=NT),
                 scalar=d_col[:, t:t + 1],
-                in1=d_all[:].rearrange("p u n -> p n u"),
+                in1=d_alls[0][:].rearrange("p u n -> p n u"),
                 op0=ALU.mult,
                 op1=ALU.mult,
             )
-        adj_grp = const.tile([P, NODES, NT], BF16, name="adj_grp", align_bytes=64)
-        nc.vector.tensor_copy(
-            out=adj_grp[:].rearrange("p (o i) t -> p o t i", i=4),
-            in_=adj_pl[:].rearrange("p t (o i) -> p o t i", i=4),
-        )
-        adj_code = const.tile([P, NODES], U32, name="adj_code", align_bytes=64)
-        adj_scale = const.tile([P, NODES], U8, name="adj_scale", align_bytes=64)
 
-        drain1(0, "ssss")
-        nc.vector.quantize_mx(
-            out=adj_code[:].bitcast(FP8X4), scales=adj_scale[:], in_=adj_grp[:].rearrange("p i t -> p (i t)")
-        )
-        quant_sup(0)
+        def rga():
+            nc.vector.tensor_copy(
+                out=adj_grp[:].rearrange("p (o i) t -> p o t i", i=4),
+                in_=adj_pl[:].rearrange("p t (o i) -> p o t i", i=4),
+            )
 
-        def stage2(n, engines):
-            res = outp.tile([P, NT, FC], F32, name="res", tag="res")
-            for it in range(NT):
-                acc = psum.tile([P, FC], F32, name="acc2", tag="s2")
-                nc.tensor.matmul_mx(
-                    out=acc[:],
-                    lhsT=adj_code[:, it * P:(it + 1) * P].bitcast(FP8X4),
-                    lhsT_scale=adj_scale[:, it * P:(it + 1) * P],
-                    rhs=sup_code[n][:].bitcast(FP8X4),
-                    rhs_scale=sup_scale[n][:],
-                    start=True,
-                    stop=True,
-                )
-                copy_on(engines[it], res[:, it, :], acc[:])
-                nc.sync.dma_start(out=out[it * P:(it + 1) * P, n * FC:(n + 1) * FC], in_=res[:, it, :])
+        def qa():
+            nc.vector.quantize_mx(
+                out=adj_code[:].bitcast(FP8X4), scales=adj_scale[:], in_=adj_grp[:].rearrange("p i t -> p (i t)")
+            )
 
-        for n in range(NCH):
-            if n + 1 < NCH:
-                stage1(n + 1)
-                drain1(n + 1, "ssss" if n + 2 < NCH else "svsv")
-            if n + 2 < NCH:
-                prep_w(n + 2)
-            stage2(n, "ssss" if n + 1 < NCH else "svsv")
-            if n + 1 < NCH:
-                quant_sup(n + 1)
+        banks1 = {}
+        sup_grp = {}
+        sup_code = {}
+        sup_scale = {}
+        banks2 = {}
+        group_of = {}
+        for g in range(len(GROUPS)):
+            for u in GROUPS[g]:
+                group_of[u] = g
+
+        def s1(u, b):
+            acc = psum.tile([P, NT, FB], F32, name="acc1", tag="s1")
+            for t in range(NT):
+                for c in range(PASSES1):
+                    nc.tensor.matmul_mx(
+                        out=acc[:, t, :],
+                        lhsT=h_code[:, t, c * P:(c + 1) * P].bitcast(FP8X4),
+                        lhsT_scale=h_scale[:, t, c * P:(c + 1) * P],
+                        rhs=w_code[u][:, c, b * FB:(b + 1) * FB].bitcast(FP8X4),
+                        rhs_scale=w_scale[u][:, c, b * FB:(b + 1) * FB],
+                        start=(c == 0),
+                        stop=(c == PASSES1 - 1),
+                    )
+            banks1[(u, b)] = acc
+
+        def co1(u, b, engine):
+            g = group_of[u]
+            if g not in sup_grp:
+                sup_grp[g] = work.tile([P, FU * len(GROUPS[g]), NT], BF16, name="sup_grp", tag="sup_grp", align_bytes=64)
+            f0 = (u - GROUPS[g][0]) * FU + b * FB
+            copy_on(engine, sup_grp[g][:, f0:f0 + FB, :], banks1[(u, b)][:].rearrange("p t f -> p f t"))
+
+        def qs(g):
+            width = FU * len(GROUPS[g])
+            code = wq.tile([P, width], U32, name="sup_code", tag="sup_code", align_bytes=64)
+            scale = wq.tile([P, width], U8, name="sup_scale", tag="sup_scale", align_bytes=64)
+            nc.vector.quantize_mx(
+                out=code[:].bitcast(FP8X4), scales=scale[:], in_=sup_grp[g][:].rearrange("p f t -> p (f t)")
+            )
+            sup_code[g] = code
+            sup_scale[g] = scale
+
+        def s2(g, it):
+            width = FU * len(GROUPS[g])
+            acc = psum.tile([P, width], F32, name="acc2", tag="s2")
+            nc.tensor.matmul_mx(
+                out=acc[:],
+                lhsT=adj_code[:, it * P:(it + 1) * P].bitcast(FP8X4),
+                lhsT_scale=adj_scale[:, it * P:(it + 1) * P],
+                rhs=sup_code[g][:].bitcast(FP8X4),
+                rhs_scale=sup_scale[g][:],
+                start=True,
+                stop=True,
+            )
+            banks2[(g, it)] = acc
+
+        def co2(g, it, engine):
+            width = FU * len(GROUPS[g])
+            f0 = GROUPS[g][0] * FU
+            res = outp.tile([P, width], F32, name="res", tag="res")
+            copy_on(engine, res[:], banks2[(g, it)][:])
+            nc.sync.dma_start(out=out[it * P:(it + 1) * P, f0:f0 + width], in_=res[:])
+
+        ts(0)
+        tt(0)
+        ts(1)
+        transp(0)
+        tt(1)
+        ts(2)
+        ts(3)
+        hco(0, 0, "s")
+        hco(0, 1, "s")
+        tt(2)
+        tt(3)
+        transp(1)
+        transp(2)
+        qh(0)
+        hco(1, 0, "s")
+        hco(1, 1, "s")
+        rg(0, "v")
+        qh(1)
+        transp(3)
+        hco(2, 0, "s")
+        hco(2, 1, "v")
+        hco(3, 0, "s")
+        hco(3, 1, "s")
+        qw(0)
+        rg(1, "v")
+        qh(2)
+        qw(1)
+        rg(2, "v")
+        rs(0)
+        rs(1)
+        rs(2)
+        rs(3)
+        sqrt()
+        rg(3, "s")
+        recip()
+        qh(3)
+        bc()
+        s1(0, 0)
+        s1(0, 1)
+        rg(4, "s")
+        qw(2)
+        rg(5, "v")
+        qw(3)
+        s1(1, 0)
+        s1(1, 1)
+        co1(0, 0, "s")
+        co1(0, 1, "s")
+        stt(0)
+        stt(1)
+        stt(2)
+        stt(3)
+        qw(4)
+        s1(2, 0)
+        s1(2, 1)
+        co1(1, 0, "s")
+        co1(1, 1, "s")
+        rga()
+        co1(2, 0, "s")
+        co1(2, 1, "s")
+        qs(0)
+        s1(3, 0)
+        s1(3, 1)
+        s1(4, 0)
+        s1(4, 1)
+        co1(3, 0, "s")
+        co1(3, 1, "s")
+        qa()
+        s2(0, 0)
+        s2(0, 1)
+        s2(0, 2)
+        s2(0, 3)
+        qw(5)
+        qs(1)
+        co1(4, 0, "s")
+        co1(4, 1, "s")
+        rg(6, "v")
+        co2(0, 0, "s")
+        co2(0, 1, "s")
+        co2(0, 2, "s")
+        co2(0, 3, "v")
+        s1(5, 0)
+        s1(5, 1)
+        qw(6)
+        co1(5, 0, "s")
+        co1(5, 1, "s")
+        rg(7, "v")
+        qs(2)
+        s2(1, 0)
+        s2(1, 1)
+        s2(1, 2)
+        s2(1, 3)
+        s1(6, 0)
+        s1(6, 1)
+        co2(1, 0, "s")
+        co2(1, 1, "s")
+        co2(1, 2, "s")
+        co2(1, 3, "v")
+        qw(7)
+        co1(6, 0, "v")
+        co1(6, 1, "s")
+        s2(2, 0)
+        s2(2, 1)
+        s2(2, 2)
+        s2(2, 3)
+        co2(2, 0, "s")
+        co2(2, 1, "s")
+        co2(2, 2, "s")
+        co2(2, 3, "v")
+        qs(3)
+        s1(7, 0)
+        s1(7, 1)
+        s2(3, 0)
+        s2(3, 1)
+        s2(3, 2)
+        s2(3, 3)
+        co1(7, 0, "s")
+        co1(7, 1, "v")
+        co2(3, 0, "s")
+        co2(3, 1, "s")
+        co2(3, 2, "s")
+        co2(3, 3, "s")
+        qs(4)
+        s2(4, 0)
+        s2(4, 1)
+        s2(4, 2)
+        s2(4, 3)
+        co2(4, 0, "s")
+        co2(4, 1, "v")
+        co2(4, 2, "s")
+        co2(4, 3, "s")

@@ -15,6 +15,7 @@ ALU = mybir.AluOpType
 
 P = 128
 PACK = 4
+PAIRS = 2
 NODES = 512
 K1 = 1024
 F2 = 2048
@@ -45,8 +46,6 @@ def tile_gcnresnet_pa_kernel(tc, x_pre, A, W_gc2, out):
             else:
                 nc.scalar.copy(out=dst, in_=src)
 
-        ident_b = const.tile([P, P], BF16, name="ident_b")
-        make_identity(nc, ident_b[:])
         ident_f = const.tile([P, P], F32, name="ident_f")
         make_identity(nc, ident_f[:])
         one = const.tile([P, 1], F32, name="one")
@@ -58,18 +57,21 @@ def tile_gcnresnet_pa_kernel(tc, x_pre, A, W_gc2, out):
         x_view = x_pre.rearrange("(p t) k -> p t k", t=NT)
         for t in range(NT):
             nc.sync.dma_start(out=x_raw[:, t, :], in_=x_view[:, t, :])
-        w_view = W_gc2.rearrange("(g p) f -> p g f", p=P)
+        w_view = W_gc2.rearrange("(c p j) f -> p c j f", p=P, j=PACK)
         a_raw = const.tile([P, NT, NODES], BF16, name="a_raw")
         w_raw = []
         for n in range(NCH):
             w_tile = wraw.tile([P, PASSES1 * PACK, FC], BF16, name="w_raw", tag="w_raw")
-            nc.sync.dma_start(out=w_tile[:], in_=w_view[:, :, n * FC:(n + 1) * FC])
+            for c in range(PASSES1):
+                nc.sync.dma_start(
+                    out=w_tile[:, c * PACK:(c + 1) * PACK, :], in_=w_view[:, c, :, n * FC:(n + 1) * FC]
+                )
             w_raw.append(w_tile)
             if n == 0:
                 nc.sync.dma_start(out=a_raw[:], in_=A.rearrange("(p t) i -> p t i", t=NT))
 
         h_nat = const.tile([P, NT, K1], BF16, name="h_nat")
-        h_grp = const.tile([P, NT, PASSES1, P, PACK], BF16, name="h_grp", align_bytes=64)
+        h_grp = const.tile([P, NT, PASSES1, P, PAIRS], F32, name="h_grp", align_bytes=64)
         h_code = const.tile([P, NT, PASSES1 * P], U32, name="h_code", align_bytes=64)
         h_scale = const.tile([P, NT, PASSES1 * P], U8, name="h_scale", align_bytes=64)
         xts = {}
@@ -84,21 +86,24 @@ def tile_gcnresnet_pa_kernel(tc, x_pre, A, W_gc2, out):
             nc.vector.tensor_max(out=h_nat[:, t, :], in0=x_raw[:, t, :], in1=scaleds[t][:])
 
         def transp(t):
+            words = h_nat[:, t, :].bitcast(F32)
+            xt = psum.tile([P, PASSES1, PAIRS, P], F32, name="xt", tag="s1" if t % 2 == 0 else "s2")
             for c in range(PASSES1):
-                xt = psum.tile([P, PACK, P], BF16, name="xt", tag="s1" if c == 0 else "s2")
-                for j in range(PACK):
-                    k0 = (c * PACK + j) * P
-                    nc.tensor.transpose(out=xt[:, j, :], in_=h_nat[:, t, k0:k0 + P], identity=ident_b[:])
-                xts[(t, c)] = xt
+                for e in range(PAIRS):
+                    w0 = c * P * PAIRS
+                    nc.tensor.transpose(
+                        out=xt[:, c, e, :], in_=words[:, w0 + e:w0 + P * PAIRS:PAIRS], identity=ident_f[:]
+                    )
+            xts[t] = xt
 
-        def hco(t, c, engine):
-            copy_on(engine, h_grp[:, t, c, :, :], xts[(t, c)][:].rearrange("p j m -> p m j"))
+        def hco(t, engine):
+            copy_on(engine, h_grp[:, t, :, :, :], xts[t][:].rearrange("p c e m -> p c m e"))
 
         def qh(t):
             nc.vector.quantize_mx(
                 out=h_code[:, t, :].bitcast(FP8X4),
                 scales=h_scale[:, t, :],
-                in_=h_grp[:, t, :, :, :].rearrange("p c m j -> p (c m j)"),
+                in_=h_grp[:, t, :, :, :].rearrange("p c m e -> p (c m e)").bitcast(BF16),
             )
 
         w_grp = {}
@@ -250,22 +255,18 @@ def tile_gcnresnet_pa_kernel(tc, x_pre, A, W_gc2, out):
         tt(1)
         ts(2)
         ts(3)
-        hco(0, 0, "s")
-        hco(0, 1, "s")
+        hco(0, "s")
         tt(2)
         tt(3)
         transp(1)
         transp(2)
         qh(0)
-        hco(1, 0, "s")
-        hco(1, 1, "s")
+        hco(1, "s")
         rg(0, "v")
         qh(1)
         transp(3)
-        hco(2, 0, "s")
-        hco(2, 1, "v")
-        hco(3, 0, "s")
-        hco(3, 1, "s")
+        hco(2, "s")
+        hco(3, "s")
         qw(0)
         rg(1, "v")
         qh(2)

@@ -35,8 +35,8 @@ def tile_gcnresnet_pa_kernel(tc, x_pre, A, W_gc2, out):
         const = ctx.enter_context(tc.tile_pool(name="const", bufs=1))
         work = ctx.enter_context(tc.tile_pool(name="work", bufs=3))
         wraw = ctx.enter_context(tc.tile_pool(name="wraw", bufs=NCH))
-        wq = ctx.enter_context(tc.tile_pool(name="wq", bufs=4))
-        outp = ctx.enter_context(tc.tile_pool(name="outp", bufs=8))
+        wq = ctx.enter_context(tc.tile_pool(name="wq", bufs=8))
+        outp = ctx.enter_context(tc.tile_pool(name="outp", bufs=20))
         psum = ctx.enter_context(tc.psum_pool(name="psum", bufs=4))
         ctx.enter_context(tc.manual_schedule())
 
@@ -55,7 +55,10 @@ def tile_gcnresnet_pa_kernel(tc, x_pre, A, W_gc2, out):
 
         x_raw = const.tile([P, NT, K1], BF16, name="x_raw")
         x_view = x_pre.rearrange("(p t) k -> p t k", t=NT)
-        for t in range(NT):
+        half = K1 // 2
+        nc.sync.dma_start(out=x_raw[:, 0, :half], in_=x_view[:, 0, :half])
+        nc.sync.dma_start(out=x_raw[:, 0, half:], in_=x_view[:, 0, half:])
+        for t in range(1, NT):
             nc.sync.dma_start(out=x_raw[:, t, :], in_=x_view[:, t, :])
         w_view = W_gc2.rearrange("(c p j) f -> p c j f", p=P, j=PACK)
         a_raw = const.tile([P, NT, NODES], BF16, name="a_raw")
@@ -77,24 +80,28 @@ def tile_gcnresnet_pa_kernel(tc, x_pre, A, W_gc2, out):
         xts = {}
         scaleds = {}
 
-        def ts(t):
-            scaled = work.tile([P, K1], BF16, name="scaled", tag="scaled")
-            nc.vector.tensor_scalar_mul(out=scaled[:], in0=x_raw[:, t, :], scalar1=SLOPE)
-            scaleds[t] = scaled
+        def ts(t, k0=0, k1=K1, engine="v"):
+            if t not in scaleds:
+                scaleds[t] = const.tile([P, K1], BF16, name="scaled_%d" % t)
+            if engine == "v":
+                nc.vector.tensor_scalar_mul(out=scaleds[t][:, k0:k1], in0=x_raw[:, t, k0:k1], scalar1=SLOPE)
+            else:
+                nc.scalar.activation(out=scaleds[t][:, k0:k1], in_=x_raw[:, t, k0:k1], func=ACT.Copy, scale=SLOPE)
 
-        def tt(t):
-            nc.vector.tensor_max(out=h_nat[:, t, :], in0=x_raw[:, t, :], in1=scaleds[t][:])
+        def tt(t, k0=0, k1=K1):
+            nc.vector.tensor_max(out=h_nat[:, t, k0:k1], in0=x_raw[:, t, k0:k1], in1=scaleds[t][:, k0:k1])
 
-        def transp(t):
+        def transp(t, passes=range(PASSES1)):
             words = h_nat[:, t, :].bitcast(F32)
-            xt = psum.tile([P, PASSES1, PAIRS, P], F32, name="xt", tag="s1" if t % 2 == 0 else "s2")
-            for c in range(PASSES1):
+            if t not in xts:
+                xts[t] = psum.tile([P, PASSES1, PAIRS, P], F32, name="xt", tag="s1" if t % 2 == 0 else "s2")
+            xt = xts[t]
+            for c in passes:
                 for e in range(PAIRS):
                     w0 = c * P * PAIRS
                     nc.tensor.transpose(
                         out=xt[:, c, e, :], in_=words[:, w0 + e:w0 + P * PAIRS:PAIRS], identity=ident_f[:]
                     )
-            xts[t] = xt
 
         def hco(t, engine):
             copy_on(engine, h_grp[:, t, :, :, :], xts[t][:].rearrange("p c e m -> p c m e"))
@@ -110,21 +117,22 @@ def tile_gcnresnet_pa_kernel(tc, x_pre, A, W_gc2, out):
         w_code = {}
         w_scale = {}
 
-        def rg(u, engine):
-            grp = work.tile([P, PASSES1, FU, PACK], BF16, name="w_grp", tag="w_grp", align_bytes=64)
-            src = w_raw[u // 2][:, :, (u % 2) * FU:(u % 2 + 1) * FU]
-            if engine == "v":
+        def rg(u, engine, passes=range(PASSES1)):
+            if u not in w_grp:
+                w_grp[u] = work.tile([P, PASSES1, FU, PACK], BF16, name="w_grp", tag="w_grp", bufs=8, align_bytes=64)
+            f0 = (u % 2) * FU
+            if engine == "v" and len(passes) == PASSES1:
                 nc.vector.tensor_copy(
-                    out=grp[:].rearrange("p c (o i) j -> p c o j i", i=4),
-                    in_=src.rearrange("p (c j) (o i) -> p c o j i", j=PACK, i=4),
+                    out=w_grp[u][:].rearrange("p c (o i) j -> p c o j i", i=4),
+                    in_=w_raw[u // 2][:, :, f0:f0 + FU].rearrange("p (c j) (o i) -> p c o j i", j=PACK, i=4),
                 )
-            else:
-                for c in range(PASSES1):
-                    nc.scalar.copy(
-                        out=grp[:, c, :, :].rearrange("p (o i) j -> p o j i", i=4),
-                        in_=src[:, c * PACK:(c + 1) * PACK, :].rearrange("p j (o i) -> p o j i", i=4),
-                    )
-            w_grp[u] = grp
+                return
+            for c in passes:
+                copy_on(
+                    engine,
+                    w_grp[u][:, c, :, :].rearrange("p (o i) j -> p o j i", i=4),
+                    w_raw[u // 2][:, c * PACK:(c + 1) * PACK, f0:f0 + FU].rearrange("p j (o i) -> p o j i", i=4),
+                )
 
         def qw(u):
             code = wq.tile([P, PASSES1, FU], U32, name="w_code", tag="w_code", align_bytes=64)
@@ -190,6 +198,7 @@ def tile_gcnresnet_pa_kernel(tc, x_pre, A, W_gc2, out):
         sup_code = {}
         sup_scale = {}
         banks2 = {}
+        stores = {}
         group_of = {}
         for g in range(len(GROUPS)):
             for u in GROUPS[g]:
@@ -213,7 +222,7 @@ def tile_gcnresnet_pa_kernel(tc, x_pre, A, W_gc2, out):
         def co1(u, b, engine):
             g = group_of[u]
             if g not in sup_grp:
-                sup_grp[g] = work.tile([P, FU * len(GROUPS[g]), NT], BF16, name="sup_grp", tag="sup_grp", align_bytes=64)
+                sup_grp[g] = work.tile([P, FU * len(GROUPS[g]), NT], BF16, name="sup_grp", tag="sup_grp", bufs=5, align_bytes=64)
             f0 = (u - GROUPS[g][0]) * FU + b * FB
             copy_on(engine, sup_grp[g][:, f0:f0 + FB, :], banks1[(u, b)][:].rearrange("p t f -> p f t"))
 
@@ -246,131 +255,161 @@ def tile_gcnresnet_pa_kernel(tc, x_pre, A, W_gc2, out):
             f0 = GROUPS[g][0] * FU
             res = outp.tile([P, width], F32, name="res", tag="res")
             copy_on(engine, res[:], banks2[(g, it)][:])
-            nc.sync.dma_start(out=out[it * P:(it + 1) * P, f0:f0 + width], in_=res[:])
+            stores[(g, it)] = (out[it * P:(it + 1) * P, f0:f0 + width], res)
 
-        ts(0)
-        tt(0)
-        ts(1)
-        transp(0)
-        tt(1)
-        ts(2)
-        ts(3)
+        def st(g, it):
+            dst, res = stores[(g, it)]
+            nc.sync.dma_start(out=dst, in_=res[:])
+
+        ts(0, 0, half)
+        ts(0, half, K1)
+        tt(0, 0, half)
+        transp(0, [0])
+        tt(0, half, K1)
+        transp(0, [1])
         hco(0, "s")
-        tt(2)
-        tt(3)
+        ts(1)
+        ts(2)
+        tt(1)
         transp(1)
-        transp(2)
-        qh(0)
         hco(1, "s")
-        rg(0, "v")
-        qh(1)
-        transp(3)
+        ts(3)
+        tt(2)
+        transp(2)
         hco(2, "s")
+        tt(3)
+        transp(3)
         hco(3, "s")
-        qw(0)
-        rg(1, "v")
-        qh(2)
-        qw(1)
-        rg(2, "v")
+        rg(0, "v", [0])
         rs(0)
+        rg(1, "v", [0])
         rs(1)
+        qh(0)
         rs(2)
+        qh(1)
         rs(3)
+        rg(0, "v", [1])
         sqrt()
+        qh(2)
         rg(3, "s")
-        recip()
         qh(3)
-        bc()
+        qw(0)
         s1(0, 0)
         s1(0, 1)
-        rg(4, "s")
-        qw(2)
-        rg(5, "v")
-        qw(3)
+        co1(0, 0, "s")
+        rg(1, "v", [1])
+        co1(0, 1, "s")
+        recip()
+        bc()
+        rg(4, "s", [0])
+        rg(2, "v")
+        qw(1)
         s1(1, 0)
         s1(1, 1)
-        co1(0, 0, "s")
-        co1(0, 1, "s")
-        stt(0)
-        stt(1)
-        stt(2)
-        stt(3)
-        qw(4)
+        co1(1, 0, "s")
+        qw(2)
         s1(2, 0)
         s1(2, 1)
-        co1(1, 0, "s")
         co1(1, 1, "s")
-        rga()
+        stt(0)
+        rg(4, "s", [1])
+        stt(1)
         co1(2, 0, "s")
+        stt(2)
         co1(2, 1, "s")
-        qs(0)
+        stt(3)
+        qw(3)
         s1(3, 0)
         s1(3, 1)
-        s1(4, 0)
-        s1(4, 1)
         co1(3, 0, "s")
+        rga()
         co1(3, 1, "s")
+        qs(0)
         qa()
         s2(0, 0)
         s2(0, 1)
         s2(0, 2)
         s2(0, 3)
-        qw(5)
-        qs(1)
-        co1(4, 0, "s")
-        co1(4, 1, "s")
-        rg(6, "v")
         co2(0, 0, "s")
+        st(0, 0)
+        rg(5, "v")
         co2(0, 1, "s")
+        st(0, 1)
+        qw(4)
+        s1(4, 0)
+        s1(4, 1)
         co2(0, 2, "s")
-        co2(0, 3, "v")
+        st(0, 2)
+        qw(5)
         s1(5, 0)
         s1(5, 1)
-        qw(6)
-        co1(5, 0, "s")
-        co1(5, 1, "s")
-        rg(7, "v")
-        qs(2)
+        co2(0, 3, "s")
+        st(0, 3)
+        qs(1)
         s2(1, 0)
         s2(1, 1)
         s2(1, 2)
         s2(1, 3)
+        co1(4, 0, "s")
+        rg(6, "v")
+        co1(4, 1, "s")
+        qw(6)
         s1(6, 0)
         s1(6, 1)
-        co2(1, 0, "s")
-        co2(1, 1, "s")
-        co2(1, 2, "s")
-        co2(1, 3, "v")
-        qw(7)
-        co1(6, 0, "v")
-        co1(6, 1, "s")
+        co1(5, 0, "s")
+        rg(7, "v")
+        co1(5, 1, "s")
+        qs(2)
         s2(2, 0)
         s2(2, 1)
         s2(2, 2)
-        s2(2, 3)
-        co2(2, 0, "s")
-        co2(2, 1, "s")
-        co2(2, 2, "s")
-        co2(2, 3, "v")
-        qs(3)
+        co2(1, 0, "s")
+        st(1, 0)
+        qw(7)
         s1(7, 0)
+        s2(2, 3)
         s1(7, 1)
+        co2(1, 1, "s")
+        st(1, 1)
+        co1(6, 0, "v")
+        co2(1, 2, "s")
+        st(1, 2)
+        co1(6, 1, "v")
+        co2(1, 3, "s")
+        st(1, 3)
+        qs(3)
         s2(3, 0)
         s2(3, 1)
         s2(3, 2)
         s2(3, 3)
+        co2(2, 0, "s")
+        st(2, 0)
+        co2(2, 2, "v")
+        co2(2, 1, "s")
+        st(2, 1)
+        st(2, 2)
+        co2(2, 3, "v")
+        st(2, 3)
         co1(7, 0, "s")
-        co1(7, 1, "v")
-        co2(3, 0, "s")
-        co2(3, 1, "s")
-        co2(3, 2, "s")
-        co2(3, 3, "s")
+        co1(7, 1, "s")
         qs(4)
         s2(4, 0)
         s2(4, 1)
         s2(4, 2)
         s2(4, 3)
+        co2(3, 0, "s")
+        st(3, 0)
+        co2(3, 1, "v")
+        co2(3, 2, "s")
+        st(3, 2)
+        st(3, 1)
+        co2(3, 3, "v")
+        st(3, 3)
         co2(4, 0, "s")
+        st(4, 0)
         co2(4, 1, "v")
+        st(4, 1)
         co2(4, 2, "s")
-        co2(4, 3, "s")
+        st(4, 2)
+        co2(4, 3, "v")
+        st(4, 3)

@@ -48,6 +48,8 @@ def tile_gcnresnet_pa_kernel(tc, x_pre, A, W_gc2, out):
 
         ident_f = const.tile([P, P], F32, name="ident_f")
         make_identity(nc, ident_f[:])
+        ident_b = const.tile([P, P], BF16, name="ident_b")
+        nc.vector.tensor_copy(out=ident_b[:], in_=ident_f[:])
         one = const.tile([P, 1], F32, name="one")
         nc.vector.memset(one[:], 1.0)
         warm = const.tile([P, 1], F32, name="warm")
@@ -146,7 +148,7 @@ def tile_gcnresnet_pa_kernel(tc, x_pre, A, W_gc2, out):
             w_scale[u] = scale
 
         rowsum = const.tile([P, NT], F32, name="rowsum")
-        junk = const.tile([P, NODES], BF16, name="junk")
+        junk = const.tile([P, P], BF16, name="junk")
         root = const.tile([P, NT], F32, name="root")
         d_col = const.tile([P, NT], F32, name="d_col")
         adj_pl = const.tile([P, NT, NODES], BF16, name="adj_pl")
@@ -155,8 +157,21 @@ def tile_gcnresnet_pa_kernel(tc, x_pre, A, W_gc2, out):
         adj_scale = const.tile([P, NODES], U8, name="adj_scale", align_bytes=64)
         d_alls = {}
 
+        folds = {}
+
+        def fold():
+            folds[0] = psum.tile([P, NT, P], F32, name="folded", tag="s1")
+            for i in range(NODES // P):
+                nc.tensor.matmul(
+                    out=folds[0][:],
+                    lhsT=ident_b[:],
+                    rhs=a_raw[:, :, i * P:(i + 1) * P],
+                    start=(i == 0),
+                    stop=(i == NODES // P - 1),
+                )
+
         def rs(t):
-            nc.scalar.activation(out=junk[:], in_=a_raw[:, t, :], func=ACT.Copy, accum_out=rowsum[:, t:t + 1])
+            nc.scalar.activation(out=junk[:], in_=folds[0][:, t, :], func=ACT.Copy, accum_out=rowsum[:, t:t + 1])
 
         def sqrt():
             nc.scalar.activation(out=root[:], in_=rowsum[:], func=ACT.Sqrt)
@@ -269,54 +284,57 @@ def tile_gcnresnet_pa_kernel(tc, x_pre, A, W_gc2, out):
         transp(0, [1])
         hco(0, "s")
         ts(1)
+        rg(1, "s", [0])
         ts(2)
         tt(1)
         transp(1)
         hco(1, "s")
         ts(3)
+        rg(1, "s", [1])
         tt(2)
         transp(2)
         hco(2, "s")
+        rg(0, "v", [0])
         tt(3)
         transp(3)
+        fold()
         hco(3, "s")
-        rg(0, "v", [0])
-        rs(0)
-        rg(1, "v", [0])
-        rs(1)
-        qh(0)
-        rs(2)
-        qh(1)
-        rs(3)
         rg(0, "v", [1])
+        rs(0)
+        qh(0)
+        rs(1)
+        qh(1)
+        rs(2)
+        qw(0)
+        rs(3)
+        qw(1)
         sqrt()
         qh(2)
         rg(3, "s")
         qh(3)
-        qw(0)
         s1(0, 0)
         s1(0, 1)
         co1(0, 0, "s")
-        rg(1, "v", [1])
+        rg(2, "v", [0])
         co1(0, 1, "s")
         recip()
         bc()
-        rg(4, "s", [0])
-        rg(2, "v")
-        qw(1)
         s1(1, 0)
         s1(1, 1)
+        rg(4, "s", [0])
+        rg(2, "v", [1])
         co1(1, 0, "s")
         qw(2)
         s1(2, 0)
         s1(2, 1)
         co1(1, 1, "s")
-        stt(0)
+        rg(5, "v", [0])
         rg(4, "s", [1])
-        stt(1)
+        stt(0)
         co1(2, 0, "s")
-        stt(2)
+        stt(1)
         co1(2, 1, "s")
+        stt(2)
         stt(3)
         qw(3)
         s1(3, 0)
@@ -332,84 +350,84 @@ def tile_gcnresnet_pa_kernel(tc, x_pre, A, W_gc2, out):
         s2(0, 3)
         co2(0, 0, "s")
         st(0, 0)
-        rg(5, "v")
-        co2(0, 1, "s")
-        st(0, 1)
+        rg(5, "v", [1])
+        co2(0, 2, "s")
+        st(0, 2)
         qw(4)
         s1(4, 0)
         s1(4, 1)
-        co2(0, 2, "s")
-        st(0, 2)
+        co2(0, 3, "s")
+        st(0, 3)
         qw(5)
         s1(5, 0)
         s1(5, 1)
-        co2(0, 3, "s")
-        st(0, 3)
+        co1(4, 0, "s")
         qs(1)
         s2(1, 0)
         s2(1, 1)
         s2(1, 2)
         s2(1, 3)
-        co1(4, 0, "s")
-        rg(6, "v")
         co1(4, 1, "s")
+        rg(6, "v")
+        co1(5, 0, "s")
+        co2(0, 1, "v")
+        st(0, 1)
+        co1(5, 1, "s")
         qw(6)
         s1(6, 0)
         s1(6, 1)
-        co1(5, 0, "s")
+        co2(1, 0, "s")
+        st(1, 0)
         rg(7, "v")
-        co1(5, 1, "s")
+        co2(1, 1, "s")
+        st(1, 1)
         qs(2)
         s2(2, 0)
         s2(2, 1)
         s2(2, 2)
-        co2(1, 0, "s")
-        st(1, 0)
-        qw(7)
-        s1(7, 0)
         s2(2, 3)
-        s1(7, 1)
-        co2(1, 1, "s")
-        st(1, 1)
-        co1(6, 0, "v")
         co2(1, 2, "s")
         st(1, 2)
-        co1(6, 1, "v")
+        qw(7)
+        s1(7, 0)
+        s1(7, 1)
         co2(1, 3, "s")
         st(1, 3)
+        co1(6, 0, "v")
+        co2(2, 1, "s")
+        st(2, 1)
+        co1(6, 1, "v")
+        co2(2, 2, "s")
+        co2(2, 0, "v")
+        st(2, 0)
+        st(2, 2)
+        co2(2, 3, "s")
+        st(2, 3)
         qs(3)
         s2(3, 0)
         s2(3, 1)
         s2(3, 2)
         s2(3, 3)
-        co2(2, 0, "s")
-        st(2, 0)
-        co2(2, 2, "v")
-        co2(2, 1, "s")
-        st(2, 1)
-        st(2, 2)
-        co2(2, 3, "v")
-        st(2, 3)
-        co1(7, 0, "s")
         co1(7, 1, "s")
+        co1(7, 0, "v")
+        co2(3, 0, "s")
+        st(3, 0)
         qs(4)
         s2(4, 0)
         s2(4, 1)
         s2(4, 2)
         s2(4, 3)
-        co2(3, 0, "s")
-        st(3, 0)
-        co2(3, 1, "v")
-        co2(3, 2, "s")
-        st(3, 2)
+        co2(3, 1, "s")
         st(3, 1)
         co2(3, 3, "v")
         st(3, 3)
+        co2(3, 2, "s")
+        st(3, 2)
+        co2(4, 1, "v")
         co2(4, 0, "s")
         st(4, 0)
-        co2(4, 1, "v")
         st(4, 1)
+        co2(4, 3, "v")
         co2(4, 2, "s")
         st(4, 2)
-        co2(4, 3, "v")
         st(4, 3)

@@ -105,6 +105,11 @@ def tile_gcnresnet_pa_kernel(tc, x_pre, A, W_gc2, out):
                         out=xt[:, c, e, :], in_=words[:, w0 + e:w0 + P * PAIRS:PAIRS], identity=ident_f[:]
                     )
 
+        def keep_busy(n):
+            acc = psum.tile([P, FC], F32, name="busy", tag="s2")
+            for _ in range(n):
+                nc.tensor.matmul(out=acc[:], lhsT=x_raw[:, 0, :P], rhs=x_raw[:, 0, :FC], start=True, stop=True)
+
         def hco(t, engine):
             copy_on(engine, h_grp[:, t, :, :, :], xts[t][:].rearrange("p c e m -> p c m e"))
 
@@ -279,24 +284,29 @@ def tile_gcnresnet_pa_kernel(tc, x_pre, A, W_gc2, out):
         ts(0, 0, half)
         ts(0, half, K1)
         tt(0, 0, half)
+        keep_busy(2)
         transp(0, [0])
         tt(0, half, K1)
         transp(0, [1])
+        keep_busy(1)
         hco(0, "s")
         ts(1)
         rg(1, "s", [0])
         ts(2)
         tt(1)
         transp(1)
+        keep_busy(1)
         hco(1, "s")
         ts(3)
         rg(1, "s", [1])
         tt(2)
         transp(2)
+        keep_busy(1)
         hco(2, "s")
         rg(0, "v", [0])
         tt(3)
         transp(3)
+        keep_busy(2)
         fold()
         hco(3, "s")
         rg(0, "v", [1])

from contextlib import ExitStack

import concourse.mybir as mybir
from concourse.masks import make_identity

FLOPS = 2 * 512 * 1024 * 2048 + 2 * 512 * 512 * 2048

BF16 = mybir.dt.bfloat16
F32 = mybir.dt.float32
U32 = mybir.dt.uint32
U8 = mybir.dt.uint8
FP8X4 = mybir.dt.float8_e4m3fn_x4
ACT = mybir.ActivationFunctionType
ALU = mybir.AluOpType

P = 128
PACK = 4
PAIRS = 2
NODES = 512
K1 = 1024
F2 = 2048
PASSES1 = K1 // (P * PACK)
NT = NODES // P
FC = 512
NCH = F2 // FC
FU = 256
FB = 128
SLOPE = 0.2
GROUPS = ((0, 1), (2, 3), (4, 5), (6,), (7,))


def tile_gcnresnet_pa_kernel(tc, x_pre, A, W_gc2, out):
    nc = tc.nc
    with ExitStack() as ctx:
        const = ctx.enter_context(tc.tile_pool(name="const", bufs=1))
        work = ctx.enter_context(tc.tile_pool(name="work", bufs=3))
        wraw = ctx.enter_context(tc.tile_pool(name="wraw", bufs=NCH))
        wq = ctx.enter_context(tc.tile_pool(name="wq", bufs=8))
        outp = ctx.enter_context(tc.tile_pool(name="outp", bufs=20))
        psum = ctx.enter_context(tc.psum_pool(name="psum", bufs=4))
        ctx.enter_context(tc.manual_schedule())

        def copy_on(engine, dst, src):
            if engine == "v":
                nc.vector.tensor_copy(out=dst, in_=src)
            else:
                nc.scalar.copy(out=dst, in_=src)

        ident_f = const.tile([P, P], F32, name="ident_f")
        make_identity(nc, ident_f[:])
        ident_b = const.tile([P, P], BF16, name="ident_b")
        nc.vector.tensor_copy(out=ident_b[:], in_=ident_f[:])
        one = const.tile([P, 1], F32, name="one")
        nc.vector.memset(one[:], 1.0)
        warm = const.tile([P, 1], F32, name="warm")
        nc.scalar.activation(out=warm[:], in_=one[:], func=ACT.Sqrt)

        x_raw = const.tile([P, NT, K1], BF16, name="x_raw")
        x_view = x_pre.rearrange("(p t) k -> p t k", t=NT)
        half = K1 // 2
        nc.sync.dma_start(out=x_raw[:, 0, :half], in_=x_view[:, 0, :half])
        nc.sync.dma_start(out=x_raw[:, 0, half:], in_=x_view[:, 0, half:])
        for t in range(1, NT):
            nc.sync.dma_start(out=x_raw[:, t, :], in_=x_view[:, t, :])
        w_view = W_gc2.rearrange("(c p j) f -> p c j f", p=P, j=PACK)
        a_raw = const.tile([P, NT, NODES], BF16, name="a_raw")
        w_raw = []
        for n in range(NCH):
            w_tile = wraw.tile([P, PASSES1 * PACK, FC], BF16, name="w_raw", tag="w_raw")
            for c in range(PASSES1):
                nc.sync.dma_start(
                    out=w_tile[:, c * PACK:(c + 1) * PACK, :], in_=w_view[:, c, :, n * FC:(n + 1) * FC]
                )
            w_raw.append(w_tile)
            if n == 0:
                nc.sync.dma_start(out=a_raw[:], in_=A.rearrange("(p t) i -> p t i", t=NT))

        h_nat = const.tile([P, NT, K1], BF16, name="h_nat")
        h_grp = const.tile([P, NT, PASSES1, P, PAIRS], F32, name="h_grp", align_bytes=64)
        h_code = const.tile([P, NT, PASSES1 * P], U32, name="h_code", align_bytes=64)
        h_scale = const.tile([P, NT, PASSES1 * P], U8, name="h_scale", align_bytes=64)
        xts = {}
        scaleds = {}

        def ts(t, k0=0, k1=K1, engine="v"):
            if t not in scaleds:
                scaleds[t] = const.tile([P, K1], BF16, name="scaled_%d" % t)
            if engine == "v":
                nc.vector.tensor_scalar_mul(out=scaleds[t][:, k0:k1], in0=x_raw[:, t, k0:k1], scalar1=SLOPE)
            else:
                nc.scalar.activation(out=scaleds[t][:, k0:k1], in_=x_raw[:, t, k0:k1], func=ACT.Copy, scale=SLOPE)

        def tt(t, k0=0, k1=K1):
            nc.vector.tensor_max(out=h_nat[:, t, k0:k1], in0=x_raw[:, t, k0:k1], in1=scaleds[t][:, k0:k1])

        def transp(t, passes=range(PASSES1)):
            words = h_nat[:, t, :].bitcast(F32)
            if t not in xts:
                xts[t] = psum.tile([P, PASSES1, PAIRS, P], F32, name="xt", tag="s1" if t % 2 == 0 else "s2")
            xt = xts[t]
            for c in passes:
                for e in range(PAIRS):
                    w0 = c * P * PAIRS
                    nc.tensor.transpose(
                        out=xt[:, c, e, :], in_=words[:, w0 + e:w0 + P * PAIRS:PAIRS], identity=ident_f[:]
                    )

        def keep_busy(n):
            acc = psum.tile([P, FC], F32, name="busy", tag="s2")
            for _ in range(n):
                nc.tensor.matmul(out=acc[:], lhsT=x_raw[:, 0, :P], rhs=x_raw[:, 0, :FC], start=True, stop=True)

        def hco(t, engine):
            copy_on(engine, h_grp[:, t, :, :, :], xts[t][:].rearrange("p c e m -> p c m e"))

        def qh(t):
            nc.vector.quantize_mx(
                out=h_code[:, t, :].bitcast(FP8X4),
                scales=h_scale[:, t, :],
                in_=h_grp[:, t, :, :, :].rearrange("p c m e -> p (c m e)").bitcast(BF16),
            )

        w_grp = {}
        w_code = {}
        w_scale = {}

        def rg(u, engine, passes=range(PASSES1)):
            if u not in w_grp:
                w_grp[u] = work.tile([P, PASSES1, FU, PACK], BF16, name="w_grp", tag="w_grp", bufs=8, align_bytes=64)
            f0 = (u % 2) * FU
            if engine == "v" and len(passes) == PASSES1:
                nc.vector.tensor_copy(
                    out=w_grp[u][:].rearrange("p c (o i) j -> p c o j i", i=4),
                    in_=w_raw[u // 2][:, :, f0:f0 + FU].rearrange("p (c j) (o i) -> p c o j i", j=PACK, i=4),
                )
                return
            for c in passes:
                copy_on(
                    engine,
                    w_grp[u][:, c, :, :].rearrange("p (o i) j -> p o j i", i=4),
                    w_raw[u // 2][:, c * PACK:(c + 1) * PACK, f0:f0 + FU].rearrange("p j (o i) -> p o j i", i=4),
                )

        def qw(u):
            code = wq.tile([P, PASSES1, FU], U32, name="w_code", tag="w_code", align_bytes=64)
            scale = wq.tile([P, PASSES1, FU], U8, name="w_scale", tag="w_scale", align_bytes=64)
            nc.vector.quantize_mx(
                out=code[:].rearrange("p c f -> p (c f)").bitcast(FP8X4),
                scales=scale[:].rearrange("p c f -> p (c f)"),
                in_=w_grp[u][:].rearrange("p c f j -> p (c f j)"),
            )
            w_code[u] = code
            w_scale[u] = scale

        rowsum = const.tile([P, NT], F32, name="rowsum")
        junk = const.tile([P, P], BF16, name="junk")
        root = const.tile([P, NT], F32, name="root")
        d_col = const.tile([P, NT], F32, name="d_col")
        adj_pl = const.tile([P, NT, NODES], BF16, name="adj_pl")
        adj_grp = const.tile([P, NODES, NT], BF16, name="adj_grp", align_bytes=64)
        adj_code = const.tile([P, NODES], U32, name="adj_code", align_bytes=64)
        adj_scale = const.tile([P, NODES], U8, name="adj_scale", align_bytes=64)
        d_alls = {}

        folds = {}

        def fold():
            folds[0] = psum.tile([P, NT, P], F32, name="folded", tag="s1")
            for i in range(NODES // P):
                nc.tensor.matmul(
                    out=folds[0][:],
                    lhsT=ident_b[:],
                    rhs=a_raw[:, :, i * P:(i + 1) * P],
                    start=(i == 0),
                    stop=(i == NODES // P - 1),
                )

        def rs(t):
            nc.scalar.activation(out=junk[:], in_=folds[0][:, t, :], func=ACT.Copy, accum_out=rowsum[:, t:t + 1])

        def sqrt():
            nc.scalar.activation(out=root[:], in_=rowsum[:], func=ACT.Sqrt)

        def recip():
            nc.vector.reciprocal(out=d_col[:], in_=root[:])

        def bc():
            d_all = psum.tile([P, NT, P], F32, name="d_all", tag="s2")
            for t in range(NT):
                nc.tensor.matmul(
                    out=d_all[:, t, :], lhsT=d_col[:, t:t + 1].to_broadcast([P, P]), rhs=ident_f[:], start=True, stop=True
                )
            d_alls[0] = d_all

        def stt(t):
            nc.vector.scalar_tensor_tensor(
                out=adj_pl[:, t, :].rearrange("p (n u) -> p n u", u=NT),
                in0=a_raw[:, t, :].rearrange("p (n u) -> p n u", u=NT),
                scalar=d_col[:, t:t + 1],
                in1=d_alls[0][:].rearrange("p u n -> p n u"),
                op0=ALU.mult,
                op1=ALU.mult,
            )

        def rga():
            nc.vector.tensor_copy(
                out=adj_grp[:].rearrange("p (o i) t -> p o t i", i=4),
                in_=adj_pl[:].rearrange("p t (o i) -> p o t i", i=4),
            )

        def qa():
            nc.vector.quantize_mx(
                out=adj_code[:].bitcast(FP8X4), scales=adj_scale[:], in_=adj_grp[:].rearrange("p i t -> p (i t)")
            )

        banks1 = {}
        sup_grp = {}
        sup_code = {}
        sup_scale = {}
        banks2 = {}
        stores = {}
        group_of = {}
        for g in range(len(GROUPS)):
            for u in GROUPS[g]:
                group_of[u] = g

        def s1(u, b):
            acc = psum.tile([P, NT, FB], F32, name="acc1", tag="s1")
            for t in range(NT):
                for c in range(PASSES1):
                    nc.tensor.matmul_mx(
                        out=acc[:, t, :],
                        lhsT=h_code[:, t, c * P:(c + 1) * P].bitcast(FP8X4),
                        lhsT_scale=h_scale[:, t, c * P:(c + 1) * P],
                        rhs=w_code[u][:, c, b * FB:(b + 1) * FB].bitcast(FP8X4),
                        rhs_scale=w_scale[u][:, c, b * FB:(b + 1) * FB],
                        start=(c == 0),
                        stop=(c == PASSES1 - 1),
                    )
            banks1[(u, b)] = acc

        def co1(u, b, engine):
            g = group_of[u]
            if g not in sup_grp:
                sup_grp[g] = work.tile([P, FU * len(GROUPS[g]), NT], BF16, name="sup_grp", tag="sup_grp", bufs=5, align_bytes=64)
            f0 = (u - GROUPS[g][0]) * FU + b * FB
            copy_on(engine, sup_grp[g][:, f0:f0 + FB, :], banks1[(u, b)][:].rearrange("p t f -> p f t"))

        def qs(g):
            width = FU * len(GROUPS[g])
            code = wq.tile([P, width], U32, name="sup_code", tag="sup_code", align_bytes=64)
            scale = wq.tile([P, width], U8, name="sup_scale", tag="sup_scale", align_bytes=64)
            nc.vector.quantize_mx(
                out=code[:].bitcast(FP8X4), scales=scale[:], in_=sup_grp[g][:].rearrange("p f t -> p (f t)")
            )
            sup_code[g] = code
            sup_scale[g] = scale

        def s2(g, it):
            width = FU * len(GROUPS[g])
            acc = psum.tile([P, width], F32, name="acc2", tag="s2")
            nc.tensor.matmul_mx(
                out=acc[:],
                lhsT=adj_code[:, it * P:(it + 1) * P].bitcast(FP8X4),
                lhsT_scale=adj_scale[:, it * P:(it + 1) * P],
                rhs=sup_code[g][:].bitcast(FP8X4),
                rhs_scale=sup_scale[g][:],
                start=True,
                stop=True,
            )
            banks2[(g, it)] = acc

        def co2(g, it, engine):
            width = FU * len(GROUPS[g])
            f0 = GROUPS[g][0] * FU
            res = outp.tile([P, width], F32, name="res", tag="res")
            copy_on(engine, res[:], banks2[(g, it)][:])
            stores[(g, it)] = (out[it * P:(it + 1) * P, f0:f0 + width], res)

        def st(g, it):
            dst, res = stores[(g, it)]
            nc.sync.dma_start(out=dst, in_=res[:])

        ts(0, 0, half)
        ts(0, half, K1)
        tt(0, 0, half)
        keep_busy(2)
        transp(0, [0])
        tt(0, half, K1)
        transp(0, [1])
        keep_busy(1)
        hco(0, "s")
        ts(1)
        rg(1, "s", [0])
        ts(2)
        tt(1)
        transp(1)
        keep_busy(1)
        hco(1, "s")
        ts(3)
        rg(1, "s", [1])
        tt(2)
        transp(2)
        keep_busy(1)
        hco(2, "s")
        rg(0, "v", [0])
        tt(3)
        transp(3)
        keep_busy(2)
        fold()
        hco(3, "s")
        rg(0, "v", [1])
        rs(0)
        qh(0)
        rs(1)
        qh(1)
        rs(2)
        qw(0)
        rs(3)
        qw(1)
        sqrt()
        qh(2)
        rg(3, "s")
        qh(3)
        s1(0, 0)
        s1(0, 1)
        co1(0, 0, "s")
        rg(2, "v", [0])
        co1(0, 1, "s")
        recip()
        bc()
        s1(1, 0)
        s1(1, 1)
        rg(4, "s", [0])
        rg(2, "v", [1])
        co1(1, 0, "s")
        qw(2)
        s1(2, 0)
        s1(2, 1)
        co1(1, 1, "s")
        rg(5, "v", [0])
        rg(4, "s", [1])
        stt(0)
        co1(2, 0, "s")
        stt(1)
        co1(2, 1, "s")
        stt(2)
        stt(3)
        qw(3)
        s1(3, 0)
        s1(3, 1)
        co1(3, 0, "s")
        rga()
        co1(3, 1, "s")
        qs(0)
        qa()
        s2(0, 0)
        s2(0, 1)
        s2(0, 2)
        s2(0, 3)
        co2(0, 0, "s")
        st(0, 0)
        rg(5, "v", [1])
        co2(0, 2, "s")
        st(0, 2)
        qw(4)
        s1(4, 0)
        s1(4, 1)
        co2(0, 3, "s")
        st(0, 3)
        qw(5)
        s1(5, 0)
        s1(5, 1)
        co1(4, 0, "s")
        qs(1)
        s2(1, 0)
        s2(1, 1)
        s2(1, 2)
        s2(1, 3)
        co1(4, 1, "s")
        rg(6, "v")
        co1(5, 0, "s")
        co2(0, 1, "v")
        st(0, 1)
        co1(5, 1, "s")
        qw(6)
        s1(6, 0)
        s1(6, 1)
        co2(1, 0, "s")
        st(1, 0)
        rg(7, "v")
        co2(1, 1, "s")
        st(1, 1)
        qs(2)
        s2(2, 0)
        s2(2, 1)
        s2(2, 2)
        s2(2, 3)
        co2(1, 2, "s")
        st(1, 2)
        qw(7)
        s1(7, 0)
        s1(7, 1)
        co2(1, 3, "s")
        st(1, 3)
        co1(6, 0, "v")
        co2(2, 1, "s")
        st(2, 1)
        co1(6, 1, "v")
        co2(2, 2, "s")
        co2(2, 0, "v")
        st(2, 0)
        st(2, 2)
        co2(2, 3, "s")
        st(2, 3)
        qs(3)
        s2(3, 0)
        s2(3, 1)
        s2(3, 2)
        s2(3, 3)
        co1(7, 1, "s")
        co1(7, 0, "v")
        co2(3, 0, "s")
        st(3, 0)
        qs(4)
        s2(4, 0)
        s2(4, 1)
        s2(4, 2)
        s2(4, 3)
        co2(3, 1, "s")
        st(3, 1)
        co2(3, 3, "v")
        st(3, 3)
        co2(3, 2, "s")
        st(3, 2)
        co2(4, 1, "v")
        co2(4, 0, "s")
        st(4, 0)
        st(4, 1)
        co2(4, 3, "v")
        co2(4, 2, "s")
        st(4, 2)
        st(4, 3)
